import numpy as np
import ml_dtypes

BF16 = ml_dtypes.bfloat16


def bf(x):
    return np.asarray(x, np.float32).astype(BF16)


def f32(x):
    return np.asarray(x, np.float32)


def f64(x):
    return np.asarray(x).astype(np.float64)


def striped(idx):
    return np.tile(idx.reshape(-1, 16).T, (8, 1))


S, D, M, N, R = 4096, 128, 128, 512, 8
EPS = 1e-12


def setup_inputs():
    mix = np.random.standard_normal((R, D)) / np.sqrt(R)
    return {'table': bf(np.random.standard_normal((S, R)) @ mix), 'w': bf((np.random.standard_normal((M, R)) @ mix).T), 'bias': f32(0.2 + 0.2 * np.random.random_sample((1,))), 'offs': striped(np.random.permutation(S)[:N])}


def reference(table, w, bias, offs):
    idx = offs[:16].T.reshape(-1)
    t = f64(table)
    h = f64(w)
    tn = t / np.sqrt(np.sum(t * t, axis=1, keepdims=True) + EPS)
    wn = h / np.sqrt(np.sum(h * h, axis=0, keepdims=True) + EPS)
    v = wn.T @ tn[idx].T + f64(bias)[0]
    return 1.0 / (1.0 + np.exp(-v))

@@ -1,0 +1,80 @@
+import concourse.mybir as mybir
+from concourse.masks import make_identity
+
+BF16, F32, U16 = mybir.dt.bfloat16, mybir.dt.float32, mybir.dt.uint16
+ACT = mybir.ActivationFunctionType
+MULT = mybir.AluOpType.mult
+
+P = 128
+S = 4096
+N = 512
+EPS = 1e-12
+BLOCKS = S // P
+CHUNK = 8
+CHUNKS = BLOCKS // CHUNK
+
+FLOPS = 2 * P * P * N
+
+
+def tile_t2gformer_mae_kernel(tc, table, w, bias, offs, out):
+    nc = tc.nc
+    with (
+        tc.tile_pool(name="held", bufs=1) as held,
+        tc.psum_pool(name="flipped", bufs=2) as flipped,
+        tc.psum_pool(name="products", bufs=1) as products,
+    ):
+        offsets = held.tile([P, N // 16], U16, name="offsets")
+        nc.sync.dma_start(offsets[:], offs)
+
+        rows = held.tile([P, BLOCKS, P], BF16, name="rows")
+        table_blocks = table.rearrange("(b p) k -> p b k", p=P)
+        for c in range(CHUNKS):
+            blocks = slice(c * CHUNK, (c + 1) * CHUNK)
+            nc.sync.dma_start(rows[:, blocks, :], table_blocks[:, blocks, :])
+
+        heads = held.tile([P, P], BF16, name="heads")
+        nc.gpsimd.dma_start(heads[:], w)
+        bias_col = held.tile([P, 1], F32, name="bias_col")
+        nc.gpsimd.dma_start(bias_col[:], bias.partition_broadcast(P))
+
+        identity = held.tile([P, P], BF16, name="identity")
+        make_identity(nc, identity[:])
+        eps_col = held.tile([P, 1], F32, name="eps_col")
+        nc.vector.memset(eps_col[:], EPS)
+        ones_col = held.tile([P, 1], F32, name="ones_col")
+        nc.vector.memset(ones_col[:], 1.0)
+
+        heads_sq = held.tile([P, P], F32, name="heads_sq")
+        nc.vector.tensor_tensor(heads_sq[:], heads[:], heads[:], MULT)
+        heads_ss = products.tile([P, 1], F32, name="heads_ss")
+        nc.tensor.matmul(heads_ss[:], heads_sq[:], ones_col[:], start=True, stop=True)
+        heads_norm = held.tile([P, 1], F32, name="heads_norm")
+        nc.scalar.activation(heads_norm[:], heads_ss[:], ACT.Sqrt, bias=eps_col[:])
+        heads_rnorm = held.tile([P, 1], F32, name="heads_rnorm")
+        nc.vector.reciprocal(heads_rnorm[:], heads_norm[:])
+
+        squares = held.tile([P, BLOCKS, P], BF16, name="squares")
+        rows_ss = held.tile([P, BLOCKS], F32, name="rows_ss")
+        rows_norm = held.tile([P, BLOCKS], F32, name="rows_norm")
+        rows_rnorm = held.tile([P, BLOCKS], F32, name="rows_rnorm")
+        unit_rows = held.tile([P, BLOCKS, P], BF16, name="unit_rows")
+        window = held.tile([P, S], BF16, name="window")
+        for c in range(CHUNKS):
+            blocks = slice(c * CHUNK, (c + 1) * CHUNK)
+            for b in range(c * CHUNK, (c + 1) * CHUNK):
+                nc.scalar.activation(
+                    squares[:, b, :], rows[:, b, :], ACT.Square, accum_out=rows_ss[:, b : b + 1]
+                )
+            nc.scalar.activation(rows_norm[:, blocks], rows_ss[:, blocks], ACT.Sqrt, bias=eps_col[:])
+            nc.vector.reciprocal(rows_rnorm[:, blocks], rows_norm[:, blocks])
+            flipped_chunk = flipped.tile([P, CHUNK * P], BF16, name="flipped_chunk")
+            for j, b in enumerate(range(c * CHUNK, (c + 1) * CHUNK)):
+                nc.vector.tensor_scalar_mul(unit_rows[:, b, :], rows[:, b, :], rows_rnorm[:, b : b + 1])
+                nc.tensor.transpose(flipped_chunk[:, j * P : (j + 1) * P], unit_rows[:, b, :], identity[:])
+            nc.vector.tensor_copy(window[:, c * CHUNK * P : (c + 1) * CHUNK * P], flipped_chunk[:])
+
+        cosines = products.tile([P, N], F32, name="cosines")
+        nc.tensor.matmul(cosines[:], heads[:], window[:].indirect(offsets[:]), start=True, stop=True)
+        probs = held.tile([P, N], F32, name="probs")
+        nc.scalar.activation(probs[:], cosines[:], ACT.Sigmoid, bias=bias_col[:], scale=heads_rnorm[:])
+        nc.sync.dma_start(out, probs[:])

@@ -10,8 +10,10 @@ S = 4096
 N = 512
 EPS = 1e-12
 BLOCKS = S // P
+LOAD = 4
 CHUNK = 8
 CHUNKS = BLOCKS // CHUNK
+HALF = CHUNK // 2
 
 FLOPS = 2 * P * P * N
 
@@ -23,19 +25,17 @@ def tile_t2gformer_mae_kernel(tc, table, w, bias, offs, out):
         tc.psum_pool(name="flipped", bufs=2) as flipped,
         tc.psum_pool(name="products", bufs=1) as products,
     ):
+        rows = held.tile([P, BLOCKS, P], BF16, name="rows")
+        table_blocks = table.rearrange("(b p) k -> p b k", p=P)
+        for first in range(0, BLOCKS, LOAD):
+            nc.sync.dma_start(rows[:, first : first + LOAD, :], table_blocks[:, first : first + LOAD, :])
         offsets = held.tile([P, N // 16], U16, name="offsets")
         nc.sync.dma_start(offsets[:], offs)
 
-        rows = held.tile([P, BLOCKS, P], BF16, name="rows")
-        table_blocks = table.rearrange("(b p) k -> p b k", p=P)
-        for c in range(CHUNKS):
-            blocks = slice(c * CHUNK, (c + 1) * CHUNK)
-            nc.sync.dma_start(rows[:, blocks, :], table_blocks[:, blocks, :])
-
         heads = held.tile([P, P], BF16, name="heads")
-        nc.gpsimd.dma_start(heads[:], w)
+        nc.scalar.dma_start(heads[:], w)
         bias_col = held.tile([P, 1], F32, name="bias_col")
-        nc.gpsimd.dma_start(bias_col[:], bias.partition_broadcast(P))
+        nc.scalar.dma_start(bias_col[:], bias.partition_broadcast(P))
 
         identity = held.tile([P, P], BF16, name="identity")
         make_identity(nc, identity[:])
@@ -43,6 +43,48 @@ def tile_t2gformer_mae_kernel(tc, table, w, bias, offs, out):
         nc.vector.memset(eps_col[:], EPS)
         ones_col = held.tile([P, 1], F32, name="ones_col")
         nc.vector.memset(ones_col[:], 1.0)
+
+        first_root = held.tile([P, 1], F32, name="first_root")
+        nc.scalar.activation(first_root[:], ones_col[:], ACT.Sqrt)
+
+        squares_s = held.tile([P, BLOCKS, P], BF16, name="squares_s")
+        squares_v = held.tile([P, BLOCKS, P], F32, name="squares_v")
+        rows_ss = held.tile([P, CHUNKS, 2, 8], F32, name="rows_ss")
+        rows_norm = held.tile([P, CHUNKS, 2, HALF], F32, name="rows_norm")
+        rows_rnorm = held.tile([P, BLOCKS], F32, name="rows_rnorm")
+        unit_rows = held.tile([P, BLOCKS, P], BF16, name="unit_rows")
+        window = held.tile([P, S], BF16, name="window")
+
+        def sums_of_squares(c):
+            for j in range(HALF):
+                b = c * CHUNK + j
+                nc.scalar.activation(
+                    squares_s[:, b, :], rows[:, b, :], ACT.Square, accum_out=rows_ss[:, c, 0, j : j + 1]
+                )
+            for j in range(HALF):
+                b = c * CHUNK + HALF + j
+                nc.vector.scalar_tensor_tensor(
+                    squares_v[:, b, :], rows[:, b, :], 1.0, rows[:, b, :], MULT, MULT,
+                    accum_out=rows_ss[:, c, 1, j : j + 1],
+                )
+
+        def normalise_and_flip(c):
+            nc.scalar.activation(rows_norm[:, c], rows_ss[:, c, :, 0:HALF], ACT.Sqrt, bias=eps_col[:])
+            nc.vector.reciprocal(
+                rows_rnorm[:, c * CHUNK : (c + 1) * CHUNK], rows_norm[:, c].rearrange("p h j -> p (h j)")
+            )
+            flipped_chunk = flipped.tile([P, CHUNK * P], BF16, name="flipped_chunk")
+            for j in range(CHUNK):
+                b = c * CHUNK + j
+                nc.vector.tensor_scalar_mul(unit_rows[:, b, :], rows[:, b, :], rows_rnorm[:, b : b + 1])
+                nc.tensor.transpose(flipped_chunk[:, j * P : (j + 1) * P], unit_rows[:, b, :], identity[:])
+            nc.vector.tensor_copy(window[:, c * CHUNK * P : (c + 1) * CHUNK * P], flipped_chunk[:])
+
+        sums_of_squares(0)
+        for c in range(CHUNKS):
+            if c + 1 < CHUNKS:
+                sums_of_squares(c + 1)
+            normalise_and_flip(c)
 
         heads_sq = held.tile([P, P], F32, name="heads_sq")
         nc.vector.tensor_tensor(heads_sq[:], heads[:], heads[:], MULT)
@@ -52,26 +94,6 @@ def tile_t2gformer_mae_kernel(tc, table, w, bias, offs, out):
         nc.scalar.activation(heads_norm[:], heads_ss[:], ACT.Sqrt, bias=eps_col[:])
         heads_rnorm = held.tile([P, 1], F32, name="heads_rnorm")
         nc.vector.reciprocal(heads_rnorm[:], heads_norm[:])
-
-        squares = held.tile([P, BLOCKS, P], BF16, name="squares")
-        rows_ss = held.tile([P, BLOCKS], F32, name="rows_ss")
-        rows_norm = held.tile([P, BLOCKS], F32, name="rows_norm")
-        rows_rnorm = held.tile([P, BLOCKS], F32, name="rows_rnorm")
-        unit_rows = held.tile([P, BLOCKS, P], BF16, name="unit_rows")
-        window = held.tile([P, S], BF16, name="window")
-        for c in range(CHUNKS):
-            blocks = slice(c * CHUNK, (c + 1) * CHUNK)
-            for b in range(c * CHUNK, (c + 1) * CHUNK):
-                nc.scalar.activation(
-                    squares[:, b, :], rows[:, b, :], ACT.Square, accum_out=rows_ss[:, b : b + 1]
-                )
-            nc.scalar.activation(rows_norm[:, blocks], rows_ss[:, blocks], ACT.Sqrt, bias=eps_col[:])
-            nc.vector.reciprocal(rows_rnorm[:, blocks], rows_norm[:, blocks])
-            flipped_chunk = flipped.tile([P, CHUNK * P], BF16, name="flipped_chunk")
-            for j, b in enumerate(range(c * CHUNK, (c + 1) * CHUNK)):
-                nc.vector.tensor_scalar_mul(unit_rows[:, b, :], rows[:, b, :], rows_rnorm[:, b : b + 1])
-                nc.tensor.transpose(flipped_chunk[:, j * P : (j + 1) * P], unit_rows[:, b, :], identity[:])
-            nc.vector.tensor_copy(window[:, c * CHUNK * P : (c + 1) * CHUNK * P], flipped_chunk[:])
 
         cosines = products.tile([P, N], F32, name="cosines")
         nc.tensor.matmul(cosines[:], heads[:], window[:].indirect(offsets[:]), start=True, stop=True)

@@ -13,7 +13,6 @@ BLOCKS = S // P
 LOAD = 4
 CHUNK = 8
 CHUNKS = BLOCKS // CHUNK
-HALF = CHUNK // 2
 
 FLOPS = 2 * P * P * N
 
@@ -47,32 +46,21 @@ def tile_t2gformer_mae_kernel(tc, table, w, bias, offs, out):
         first_root = held.tile([P, 1], F32, name="first_root")
         nc.scalar.activation(first_root[:], ones_col[:], ACT.Sqrt)
 
-        squares_s = held.tile([P, BLOCKS, P], BF16, name="squares_s")
-        squares_v = held.tile([P, BLOCKS, P], F32, name="squares_v")
-        rows_ss = held.tile([P, CHUNKS, 2, 8], F32, name="rows_ss")
-        rows_norm = held.tile([P, CHUNKS, 2, HALF], F32, name="rows_norm")
+        squares = held.tile([P, BLOCKS, P], BF16, name="squares")
+        rows_ss = held.tile([P, BLOCKS], F32, name="rows_ss")
+        rows_norm = held.tile([P, BLOCKS], F32, name="rows_norm")
         rows_rnorm = held.tile([P, BLOCKS], F32, name="rows_rnorm")
         unit_rows = held.tile([P, BLOCKS, P], BF16, name="unit_rows")
         window = held.tile([P, S], BF16, name="window")
 
-        def sums_of_squares(c):
-            for j in range(HALF):
-                b = c * CHUNK + j
-                nc.scalar.activation(
-                    squares_s[:, b, :], rows[:, b, :], ACT.Square, accum_out=rows_ss[:, c, 0, j : j + 1]
-                )
-            for j in range(HALF):
-                b = c * CHUNK + HALF + j
-                nc.vector.scalar_tensor_tensor(
-                    squares_v[:, b, :], rows[:, b, :], 1.0, rows[:, b, :], MULT, MULT,
-                    accum_out=rows_ss[:, c, 1, j : j + 1],
-                )
-
         def normalise_and_flip(c):
-            nc.scalar.activation(rows_norm[:, c], rows_ss[:, c, :, 0:HALF], ACT.Sqrt, bias=eps_col[:])
-            nc.vector.reciprocal(
-                rows_rnorm[:, c * CHUNK : (c + 1) * CHUNK], rows_norm[:, c].rearrange("p h j -> p (h j)")
-            )
+            blocks = slice(c * CHUNK, (c + 1) * CHUNK)
+            for b in range(c * CHUNK, (c + 1) * CHUNK):
+                nc.scalar.activation(
+                    squares[:, b, :], rows[:, b, :], ACT.Square, accum_out=rows_ss[:, b : b + 1]
+                )
+            nc.scalar.activation(rows_norm[:, blocks], rows_ss[:, blocks], ACT.Sqrt, bias=eps_col[:])
+            nc.vector.reciprocal(rows_rnorm[:, blocks], rows_norm[:, blocks])
             flipped_chunk = flipped.tile([P, CHUNK * P], BF16, name="flipped_chunk")
             for j in range(CHUNK):
                 b = c * CHUNK + j
@@ -80,10 +68,7 @@ def tile_t2gformer_mae_kernel(tc, table, w, bias, offs, out):
                 nc.tensor.transpose(flipped_chunk[:, j * P : (j + 1) * P], unit_rows[:, b, :], identity[:])
             nc.vector.tensor_copy(window[:, c * CHUNK * P : (c + 1) * CHUNK * P], flipped_chunk[:])
 
-        sums_of_squares(0)
         for c in range(CHUNKS):
-            if c + 1 < CHUNKS:
-                sums_of_squares(c + 1)
             normalise_and_flip(c)
 
         heads_sq = held.tile([P, P], F32, name="heads_sq")

@@ -11,8 +11,11 @@ N = 512
 EPS = 1e-12
 BLOCKS = S // P
 LOAD = 4
-CHUNK = 8
-CHUNKS = BLOCKS // CHUNK
+BANK = 8
+CHUNK_SIZES = (BANK, BANK, BANK, BANK // 2, BANK // 2)
+assert sum(CHUNK_SIZES) == BLOCKS
+VECTOR_CHUNK = 1
+PIECES = 2
 
 FLOPS = 2 * P * P * N
 
@@ -46,30 +49,38 @@ def tile_t2gformer_mae_kernel(tc, table, w, bias, offs, out):
         first_root = held.tile([P, 1], F32, name="first_root")
         nc.scalar.activation(first_root[:], ones_col[:], ACT.Sqrt)
 
-        squares = held.tile([P, BLOCKS, P], BF16, name="squares")
+        squares_s = held.tile([P, BLOCKS, P], BF16, name="squares_s")
+        squares_v = held.tile([P, BLOCKS, P], F32, name="squares_v")
         rows_ss = held.tile([P, BLOCKS], F32, name="rows_ss")
         rows_norm = held.tile([P, BLOCKS], F32, name="rows_norm")
         rows_rnorm = held.tile([P, BLOCKS], F32, name="rows_rnorm")
         unit_rows = held.tile([P, BLOCKS, P], BF16, name="unit_rows")
         window = held.tile([P, S], BF16, name="window")
 
-        def normalise_and_flip(c):
-            blocks = slice(c * CHUNK, (c + 1) * CHUNK)
-            for b in range(c * CHUNK, (c + 1) * CHUNK):
-                nc.scalar.activation(
-                    squares[:, b, :], rows[:, b, :], ACT.Square, accum_out=rows_ss[:, b : b + 1]
-                )
+        chunk_starts = [sum(CHUNK_SIZES[:c]) for c in range(len(CHUNK_SIZES))]
+
+        first = chunk_starts[VECTOR_CHUNK]
+        for b in range(first, first + CHUNK_SIZES[VECTOR_CHUNK]):
+            nc.vector.scalar_tensor_tensor(
+                squares_v[:, b, :], rows[:, b, :], 1.0, rows[:, b, :], MULT, MULT,
+                accum_out=rows_ss[:, b : b + 1],
+            )
+
+        for c, (first, size) in enumerate(zip(chunk_starts, CHUNK_SIZES)):
+            blocks = slice(first, first + size)
+            if c != VECTOR_CHUNK:
+                for b in range(first, first + size):
+                    nc.scalar.activation(
+                        squares_s[:, b, :], rows[:, b, :], ACT.Square, accum_out=rows_ss[:, b : b + 1]
+                    )
             nc.scalar.activation(rows_norm[:, blocks], rows_ss[:, blocks], ACT.Sqrt, bias=eps_col[:])
             nc.vector.reciprocal(rows_rnorm[:, blocks], rows_norm[:, blocks])
-            flipped_chunk = flipped.tile([P, CHUNK * P], BF16, name="flipped_chunk")
-            for j in range(CHUNK):
-                b = c * CHUNK + j
+            flipped_chunk = flipped.tile([P, size * P], BF16, name="flipped_chunk", tag="flipped_chunk")
+            for j in range(size):
+                b = first + j
                 nc.vector.tensor_scalar_mul(unit_rows[:, b, :], rows[:, b, :], rows_rnorm[:, b : b + 1])
                 nc.tensor.transpose(flipped_chunk[:, j * P : (j + 1) * P], unit_rows[:, b, :], identity[:])
-            nc.vector.tensor_copy(window[:, c * CHUNK * P : (c + 1) * CHUNK * P], flipped_chunk[:])
-
-        for c in range(CHUNKS):
-            normalise_and_flip(c)
+            nc.vector.tensor_copy(window[:, first * P : (first + size) * P], flipped_chunk[:])
 
         heads_sq = held.tile([P, P], F32, name="heads_sq")
         nc.vector.tensor_tensor(heads_sq[:], heads[:], heads[:], MULT)
@@ -80,8 +91,14 @@ def tile_t2gformer_mae_kernel(tc, table, w, bias, offs, out):
         heads_rnorm = held.tile([P, 1], F32, name="heads_rnorm")
         nc.vector.reciprocal(heads_rnorm[:], heads_norm[:])
 
-        cosines = products.tile([P, N], F32, name="cosines")
-        nc.tensor.matmul(cosines[:], heads[:], window[:].indirect(offsets[:]), start=True, stop=True)
+        width = N // PIECES
         probs = held.tile([P, N], F32, name="probs")
-        nc.scalar.activation(probs[:], cosines[:], ACT.Sigmoid, bias=bias_col[:], scale=heads_rnorm[:])
-        nc.sync.dma_start(out, probs[:])
+        for i, queue in zip(range(PIECES), (nc.sync, nc.scalar)):
+            columns = slice(i * width, (i + 1) * width)
+            cosines = products.tile([P, width], F32, name=f"cosines{i}")
+            looked_up = window[:].indirect(offsets[:, i * width // 16 : (i + 1) * width // 16])
+            nc.tensor.matmul(cosines[:], heads[:], looked_up, start=True, stop=True)
+            nc.scalar.activation(
+                probs[:, columns], cosines[:], ACT.Sigmoid, bias=bias_col[:], scale=heads_rnorm[:]
+            )
+            queue.dma_start(out[:, columns], probs[:, columns])

@@ -11,11 +11,8 @@ N = 512
 EPS = 1e-12
 BLOCKS = S // P
 LOAD = 4
-BANK = 8
-CHUNK_SIZES = (BANK, BANK, BANK, BANK // 2, BANK // 2)
-assert sum(CHUNK_SIZES) == BLOCKS
-VECTOR_CHUNK = 1
-PIECES = 2
+CHUNK = 8
+CHUNKS = BLOCKS // CHUNK
 
 FLOPS = 2 * P * P * N
 
@@ -49,38 +46,32 @@ def tile_t2gformer_mae_kernel(tc, table, w, bias, offs, out):
         first_root = held.tile([P, 1], F32, name="first_root")
         nc.scalar.activation(first_root[:], ones_col[:], ACT.Sqrt)
 
-        squares_s = held.tile([P, BLOCKS, P], BF16, name="squares_s")
-        squares_v = held.tile([P, BLOCKS, P], F32, name="squares_v")
+        squares = held.tile([P, BLOCKS, P], BF16, name="squares")
         rows_ss = held.tile([P, BLOCKS], F32, name="rows_ss")
         rows_norm = held.tile([P, BLOCKS], F32, name="rows_norm")
         rows_rnorm = held.tile([P, BLOCKS], F32, name="rows_rnorm")
         unit_rows = held.tile([P, BLOCKS, P], BF16, name="unit_rows")
         window = held.tile([P, S], BF16, name="window")
 
-        chunk_starts = [sum(CHUNK_SIZES[:c]) for c in range(len(CHUNK_SIZES))]
-
-        first = chunk_starts[VECTOR_CHUNK]
-        for b in range(first, first + CHUNK_SIZES[VECTOR_CHUNK]):
-            nc.vector.scalar_tensor_tensor(
-                squares_v[:, b, :], rows[:, b, :], 1.0, rows[:, b, :], MULT, MULT,
-                accum_out=rows_ss[:, b : b + 1],
-            )
-
-        for c, (first, size) in enumerate(zip(chunk_starts, CHUNK_SIZES)):
-            blocks = slice(first, first + size)
-            if c != VECTOR_CHUNK:
-                for b in range(first, first + size):
-                    nc.scalar.activation(
-                        squares_s[:, b, :], rows[:, b, :], ACT.Square, accum_out=rows_ss[:, b : b + 1]
-                    )
+        def normalise_and_flip(c):
+            blocks = slice(c * CHUNK, (c + 1) * CHUNK)
+            for b in range(c * CHUNK, (c + 1) * CHUNK):
+                nc.scalar.activation(
+                    squares[:, b, :], rows[:, b, :], ACT.Square, accum_out=rows_ss[:, b : b + 1]
+                )
             nc.scalar.activation(rows_norm[:, blocks], rows_ss[:, blocks], ACT.Sqrt, bias=eps_col[:])
             nc.vector.reciprocal(rows_rnorm[:, blocks], rows_norm[:, blocks])
-            flipped_chunk = flipped.tile([P, size * P], BF16, name="flipped_chunk", tag="flipped_chunk")
-            for j in range(size):
-                b = first + j
+            flipped_chunk = flipped.tile([P, CHUNK * P], BF16, name="flipped_chunk")
+            for j in range(CHUNK):
+                b = c * CHUNK + j
                 nc.vector.tensor_scalar_mul(unit_rows[:, b, :], rows[:, b, :], rows_rnorm[:, b : b + 1])
-                nc.tensor.transpose(flipped_chunk[:, j * P : (j + 1) * P], unit_rows[:, b, :], identity[:])
-            nc.vector.tensor_copy(window[:, first * P : (first + size) * P], flipped_chunk[:])
+                nc.tensor.matmul(
+                    flipped_chunk[:, j * P : (j + 1) * P], unit_rows[:, b, :], identity[:], start=True, stop=True
+                )
+            nc.vector.tensor_copy(window[:, c * CHUNK * P : (c + 1) * CHUNK * P], flipped_chunk[:])
+
+        for c in range(CHUNKS):
+            normalise_and_flip(c)
 
         heads_sq = held.tile([P, P], F32, name="heads_sq")
         nc.vector.tensor_tensor(heads_sq[:], heads[:], heads[:], MULT)
@@ -91,14 +82,8 @@ def tile_t2gformer_mae_kernel(tc, table, w, bias, offs, out):
         heads_rnorm = held.tile([P, 1], F32, name="heads_rnorm")
         nc.vector.reciprocal(heads_rnorm[:], heads_norm[:])
 
-        width = N // PIECES
+        cosines = products.tile([P, N], F32, name="cosines")
+        nc.tensor.matmul(cosines[:], heads[:], window[:].indirect(offsets[:]), start=True, stop=True)
         probs = held.tile([P, N], F32, name="probs")
-        for i, queue in zip(range(PIECES), (nc.sync, nc.scalar)):
-            columns = slice(i * width, (i + 1) * width)
-            cosines = products.tile([P, width], F32, name=f"cosines{i}")
-            looked_up = window[:].indirect(offsets[:, i * width // 16 : (i + 1) * width // 16])
-            nc.tensor.matmul(cosines[:], heads[:], looked_up, start=True, stop=True)
-            nc.scalar.activation(
-                probs[:, columns], cosines[:], ACT.Sigmoid, bias=bias_col[:], scale=heads_rnorm[:]
-            )
-            queue.dma_start(out[:, columns], probs[:, columns])
+        nc.scalar.activation(probs[:], cosines[:], ACT.Sigmoid, bias=bias_col[:], scale=heads_rnorm[:])
+        nc.sync.dma_start(out, probs[:])

@@ -13,6 +13,7 @@ BLOCKS = S // P
 LOAD = 4
 CHUNK = 8
 CHUNKS = BLOCKS // CHUNK
+WARM_UP = 7
 
 FLOPS = 2 * P * P * N
 
@@ -45,6 +46,12 @@ def tile_t2gformer_mae_kernel(tc, table, w, bias, offs, out):
 
         first_root = held.tile([P, 1], F32, name="first_root")
         nc.scalar.activation(first_root[:], ones_col[:], ACT.Sqrt)
+
+        idle_in = held.tile([P, N], BF16, name="idle_in")
+        nc.vector.memset(idle_in[:], 0.0)
+        idle_out = products.tile([P, N], F32, name="idle_out")
+        for i in range(WARM_UP):
+            nc.tensor.matmul(idle_out[:], identity[:], idle_in[:], start=True, stop=True)
 
         squares = held.tile([P, BLOCKS, P], BF16, name="squares")
         rows_ss = held.tile([P, BLOCKS], F32, name="rows_ss")

@@ -11,9 +11,9 @@ N = 512
 EPS = 1e-12
 BLOCKS = S // P
 LOAD = 4
-CHUNK = 8
-CHUNKS = BLOCKS // CHUNK
-WARM_UP = 7
+BANK = 8
+CHUNK_SIZES = (BANK, BANK, BANK, BANK // 2, BANK // 2)
+assert sum(CHUNK_SIZES) == BLOCKS
 
 FLOPS = 2 * P * P * N
 
@@ -45,49 +45,40 @@ def tile_t2gformer_mae_kernel(tc, table, w, bias, offs, out):
         nc.vector.memset(ones_col[:], 1.0)
 
         first_root = held.tile([P, 1], F32, name="first_root")
-        nc.scalar.activation(first_root[:], ones_col[:], ACT.Sqrt)
-
-        idle_in = held.tile([P, N], BF16, name="idle_in")
-        nc.vector.memset(idle_in[:], 0.0)
-        idle_out = products.tile([P, N], F32, name="idle_out")
-        for i in range(WARM_UP):
-            nc.tensor.matmul(idle_out[:], identity[:], idle_in[:], start=True, stop=True)
+        nc.scalar.activation(first_root[:], ones_col[:], ACT.Abs_reciprocal_sqrt)
 
         squares = held.tile([P, BLOCKS, P], BF16, name="squares")
         rows_ss = held.tile([P, BLOCKS], F32, name="rows_ss")
-        rows_norm = held.tile([P, BLOCKS], F32, name="rows_norm")
         rows_rnorm = held.tile([P, BLOCKS], F32, name="rows_rnorm")
         unit_rows = held.tile([P, BLOCKS, P], BF16, name="unit_rows")
         window = held.tile([P, S], BF16, name="window")
 
-        def normalise_and_flip(c):
-            blocks = slice(c * CHUNK, (c + 1) * CHUNK)
-            for b in range(c * CHUNK, (c + 1) * CHUNK):
+        first = 0
+        for size in CHUNK_SIZES:
+            blocks = slice(first, first + size)
+            for b in range(first, first + size):
                 nc.scalar.activation(
                     squares[:, b, :], rows[:, b, :], ACT.Square, accum_out=rows_ss[:, b : b + 1]
                 )
-            nc.scalar.activation(rows_norm[:, blocks], rows_ss[:, blocks], ACT.Sqrt, bias=eps_col[:])
-            nc.vector.reciprocal(rows_rnorm[:, blocks], rows_norm[:, blocks])
-            flipped_chunk = flipped.tile([P, CHUNK * P], BF16, name="flipped_chunk")
-            for j in range(CHUNK):
-                b = c * CHUNK + j
+            nc.scalar.activation(
+                rows_rnorm[:, blocks], rows_ss[:, blocks], ACT.Abs_reciprocal_sqrt, bias=eps_col[:]
+            )
+            flipped_chunk = flipped.tile([P, size * P], BF16, name="flipped_chunk", tag="flipped_chunk")
+            for j in range(size):
+                b = first + j
                 nc.vector.tensor_scalar_mul(unit_rows[:, b, :], rows[:, b, :], rows_rnorm[:, b : b + 1])
                 nc.tensor.matmul(
                     flipped_chunk[:, j * P : (j + 1) * P], unit_rows[:, b, :], identity[:], start=True, stop=True
                 )
-            nc.vector.tensor_copy(window[:, c * CHUNK * P : (c + 1) * CHUNK * P], flipped_chunk[:])
-
-        for c in range(CHUNKS):
-            normalise_and_flip(c)
+            nc.vector.tensor_copy(window[:, first * P : (first + size) * P], flipped_chunk[:])
+            first += size
 
         heads_sq = held.tile([P, P], F32, name="heads_sq")
         nc.vector.tensor_tensor(heads_sq[:], heads[:], heads[:], MULT)
         heads_ss = products.tile([P, 1], F32, name="heads_ss")
         nc.tensor.matmul(heads_ss[:], heads_sq[:], ones_col[:], start=True, stop=True)
-        heads_norm = held.tile([P, 1], F32, name="heads_norm")
-        nc.scalar.activation(heads_norm[:], heads_ss[:], ACT.Sqrt, bias=eps_col[:])
         heads_rnorm = held.tile([P, 1], F32, name="heads_rnorm")
-        nc.vector.reciprocal(heads_rnorm[:], heads_norm[:])
+        nc.scalar.activation(heads_rnorm[:], heads_ss[:], ACT.Abs_reciprocal_sqrt, bias=eps_col[:])
 
         cosines = products.tile([P, N], F32, name="cosines")
         nc.tensor.matmul(cosines[:], heads[:], window[:].indirect(offsets[:]), start=True, stop=True)

@@ -10,10 +10,8 @@ S = 4096
 N = 512
 EPS = 1e-12
 BLOCKS = S // P
-LOAD = 4
-BANK = 8
-CHUNK_SIZES = (BANK, BANK, BANK, BANK // 2, BANK // 2)
-assert sum(CHUNK_SIZES) == BLOCKS
+CHUNK = 4
+CHUNKS = BLOCKS // CHUNK
 
 FLOPS = 2 * P * P * N
 
@@ -22,13 +20,14 @@ def tile_t2gformer_mae_kernel(tc, table, w, bias, offs, out):
     nc = tc.nc
     with (
         tc.tile_pool(name="held", bufs=1) as held,
-        tc.psum_pool(name="flipped", bufs=2) as flipped,
+        tc.psum_pool(name="flipped", bufs=4) as flipped,
         tc.psum_pool(name="products", bufs=1) as products,
     ):
         rows = held.tile([P, BLOCKS, P], BF16, name="rows")
         table_blocks = table.rearrange("(b p) k -> p b k", p=P)
-        for first in range(0, BLOCKS, LOAD):
-            nc.sync.dma_start(rows[:, first : first + LOAD, :], table_blocks[:, first : first + LOAD, :])
+        for c in range(CHUNKS):
+            blocks = slice(c * CHUNK, (c + 1) * CHUNK)
+            nc.sync.dma_start(rows[:, blocks, :], table_blocks[:, blocks, :])
         offsets = held.tile([P, N // 16], U16, name="offsets")
         nc.sync.dma_start(offsets[:], offs)
 
@@ -45,40 +44,40 @@ def tile_t2gformer_mae_kernel(tc, table, w, bias, offs, out):
         nc.vector.memset(ones_col[:], 1.0)
 
         first_root = held.tile([P, 1], F32, name="first_root")
-        nc.scalar.activation(first_root[:], ones_col[:], ACT.Abs_reciprocal_sqrt)
+        nc.scalar.activation(first_root[:], ones_col[:], ACT.Sqrt)
 
         squares = held.tile([P, BLOCKS, P], BF16, name="squares")
         rows_ss = held.tile([P, BLOCKS], F32, name="rows_ss")
+        rows_norm = held.tile([P, BLOCKS], F32, name="rows_norm")
         rows_rnorm = held.tile([P, BLOCKS], F32, name="rows_rnorm")
         unit_rows = held.tile([P, BLOCKS, P], BF16, name="unit_rows")
         window = held.tile([P, S], BF16, name="window")
 
-        first = 0
-        for size in CHUNK_SIZES:
-            blocks = slice(first, first + size)
-            for b in range(first, first + size):
+        for c in range(CHUNKS):
+            blocks = slice(c * CHUNK, (c + 1) * CHUNK)
+            for b in range(c * CHUNK, (c + 1) * CHUNK):
                 nc.scalar.activation(
                     squares[:, b, :], rows[:, b, :], ACT.Square, accum_out=rows_ss[:, b : b + 1]
                 )
-            nc.scalar.activation(
-                rows_rnorm[:, blocks], rows_ss[:, blocks], ACT.Abs_reciprocal_sqrt, bias=eps_col[:]
-            )
-            flipped_chunk = flipped.tile([P, size * P], BF16, name="flipped_chunk", tag="flipped_chunk")
-            for j in range(size):
-                b = first + j
+            nc.scalar.activation(rows_norm[:, blocks], rows_ss[:, blocks], ACT.Sqrt, bias=eps_col[:])
+            nc.vector.reciprocal(rows_rnorm[:, blocks], rows_norm[:, blocks])
+            flipped_chunk = flipped.tile([P, CHUNK * P], BF16, name="flipped_chunk")
+            for j in range(CHUNK):
+                b = c * CHUNK + j
                 nc.vector.tensor_scalar_mul(unit_rows[:, b, :], rows[:, b, :], rows_rnorm[:, b : b + 1])
                 nc.tensor.matmul(
                     flipped_chunk[:, j * P : (j + 1) * P], unit_rows[:, b, :], identity[:], start=True, stop=True
                 )
-            nc.vector.tensor_copy(window[:, first * P : (first + size) * P], flipped_chunk[:])
-            first += size
+            nc.vector.tensor_copy(window[:, c * CHUNK * P : (c + 1) * CHUNK * P], flipped_chunk[:])
 
         heads_sq = held.tile([P, P], F32, name="heads_sq")
         nc.vector.tensor_tensor(heads_sq[:], heads[:], heads[:], MULT)
         heads_ss = products.tile([P, 1], F32, name="heads_ss")
         nc.tensor.matmul(heads_ss[:], heads_sq[:], ones_col[:], start=True, stop=True)
+        heads_norm = held.tile([P, 1], F32, name="heads_norm")
+        nc.scalar.activation(heads_norm[:], heads_ss[:], ACT.Sqrt, bias=eps_col[:])
         heads_rnorm = held.tile([P, 1], F32, name="heads_rnorm")
-        nc.scalar.activation(heads_rnorm[:], heads_ss[:], ACT.Abs_reciprocal_sqrt, bias=eps_col[:])
+        nc.vector.reciprocal(heads_rnorm[:], heads_norm[:])
 
         cosines = products.tile([P, N], F32, name="cosines")
         nc.tensor.matmul(cosines[:], heads[:], window[:].indirect(offsets[:]), start=True, stop=True)

@@ -12,6 +12,7 @@ EPS = 1e-12
 BLOCKS = S // P
 CHUNK = 4
 CHUNKS = BLOCKS // CHUNK
+PIECE = 128
 
 FLOPS = 2 * P * P * N
 
@@ -22,6 +23,7 @@ def tile_t2gformer_mae_kernel(tc, table, w, bias, offs, out):
         tc.tile_pool(name="held", bufs=1) as held,
         tc.psum_pool(name="flipped", bufs=4) as flipped,
         tc.psum_pool(name="products", bufs=1) as products,
+        tc.psum_pool(name="pieces", bufs=3) as pieces,
     ):
         rows = held.tile([P, BLOCKS, P], BF16, name="rows")
         table_blocks = table.rearrange("(b p) k -> p b k", p=P)
@@ -79,8 +81,18 @@ def tile_t2gformer_mae_kernel(tc, table, w, bias, offs, out):
         heads_rnorm = held.tile([P, 1], F32, name="heads_rnorm")
         nc.vector.reciprocal(heads_rnorm[:], heads_norm[:])
 
-        cosines = products.tile([P, N], F32, name="cosines")
-        nc.tensor.matmul(cosines[:], heads[:], window[:].indirect(offsets[:]), start=True, stop=True)
         probs = held.tile([P, N], F32, name="probs")
-        nc.scalar.activation(probs[:], cosines[:], ACT.Sigmoid, bias=bias_col[:], scale=heads_rnorm[:])
-        nc.sync.dma_start(out, probs[:])
+        for i in range(N // PIECE):
+            columns = slice(i * PIECE, (i + 1) * PIECE)
+            cosines = pieces.tile([P, PIECE], F32, name="cosines")
+            nc.tensor.matmul(
+                cosines[:],
+                heads[:],
+                window[:].indirect(offsets[:, i * (PIECE // 16) : (i + 1) * (PIECE // 16)]),
+                start=True,
+                stop=True,
+            )
+            nc.scalar.activation(
+                probs[:, columns], cosines[:], ACT.Sigmoid, bias=bias_col[:], scale=heads_rnorm[:]
+            )
+            nc.sync.dma_start(out[:, columns], probs[:, columns])

@@ -12,6 +12,7 @@ EPS = 1e-12
 BLOCKS = S // P
 CHUNK = 4
 CHUNKS = BLOCKS // CHUNK
+VECTOR_CHUNKS = 1
 PIECE = 128
 
 FLOPS = 2 * P * P * N
@@ -46,11 +47,10 @@ def tile_t2gformer_mae_kernel(tc, table, w, bias, offs, out):
         nc.vector.memset(ones_col[:], 1.0)
 
         first_root = held.tile([P, 1], F32, name="first_root")
-        nc.scalar.activation(first_root[:], ones_col[:], ACT.Sqrt)
+        nc.scalar.activation(first_root[:], ones_col[:], ACT.Abs_reciprocal_sqrt)
 
         squares = held.tile([P, BLOCKS, P], BF16, name="squares")
         rows_ss = held.tile([P, BLOCKS], F32, name="rows_ss")
-        rows_norm = held.tile([P, BLOCKS], F32, name="rows_norm")
         rows_rnorm = held.tile([P, BLOCKS], F32, name="rows_rnorm")
         unit_rows = held.tile([P, BLOCKS, P], BF16, name="unit_rows")
         window = held.tile([P, S], BF16, name="window")
@@ -58,11 +58,18 @@ def tile_t2gformer_mae_kernel(tc, table, w, bias, offs, out):
         for c in range(CHUNKS):
             blocks = slice(c * CHUNK, (c + 1) * CHUNK)
             for b in range(c * CHUNK, (c + 1) * CHUNK):
-                nc.scalar.activation(
-                    squares[:, b, :], rows[:, b, :], ACT.Square, accum_out=rows_ss[:, b : b + 1]
-                )
-            nc.scalar.activation(rows_norm[:, blocks], rows_ss[:, blocks], ACT.Sqrt, bias=eps_col[:])
-            nc.vector.reciprocal(rows_rnorm[:, blocks], rows_norm[:, blocks])
+                if c < CHUNKS - VECTOR_CHUNKS:
+                    nc.scalar.activation(
+                        squares[:, b, :], rows[:, b, :], ACT.Square, accum_out=rows_ss[:, b : b + 1]
+                    )
+                else:
+                    nc.vector.scalar_tensor_tensor(
+                        squares[:, b, :], rows[:, b, :], 1.0, rows[:, b, :], MULT, MULT,
+                        accum_out=rows_ss[:, b : b + 1],
+                    )
+            nc.scalar.activation(
+                rows_rnorm[:, blocks], rows_ss[:, blocks], ACT.Abs_reciprocal_sqrt, bias=eps_col[:]
+            )
             flipped_chunk = flipped.tile([P, CHUNK * P], BF16, name="flipped_chunk")
             for j in range(CHUNK):
                 b = c * CHUNK + j
@@ -76,10 +83,8 @@ def tile_t2gformer_mae_kernel(tc, table, w, bias, offs, out):
         nc.vector.tensor_tensor(heads_sq[:], heads[:], heads[:], MULT)
         heads_ss = products.tile([P, 1], F32, name="heads_ss")
         nc.tensor.matmul(heads_ss[:], heads_sq[:], ones_col[:], start=True, stop=True)
-        heads_norm = held.tile([P, 1], F32, name="heads_norm")
-        nc.scalar.activation(heads_norm[:], heads_ss[:], ACT.Sqrt, bias=eps_col[:])
         heads_rnorm = held.tile([P, 1], F32, name="heads_rnorm")
-        nc.vector.reciprocal(heads_rnorm[:], heads_norm[:])
+        nc.scalar.activation(heads_rnorm[:], heads_ss[:], ACT.Abs_reciprocal_sqrt, bias=eps_col[:])
 
         probs = held.tile([P, N], F32, name="probs")
         for i in range(N // PIECE):

@@ -1,15 +1,16 @@
 import concourse.mybir as mybir
-from concourse.masks import make_identity
 
 BF16, F32, U16 = mybir.dt.bfloat16, mybir.dt.float32, mybir.dt.uint16
 ACT = mybir.ActivationFunctionType
 MULT = mybir.AluOpType.mult
+NOT_EQUAL = mybir.AluOpType.not_equal
 
 P = 128
 S = 4096
 N = 512
 EPS = 1e-12
 BLOCKS = S // P
+PAIR = 2
 CHUNK = 4
 CHUNKS = BLOCKS // CHUNK
 VECTOR_CHUNKS = 1
@@ -27,10 +28,11 @@ def tile_t2gformer_mae_kernel(tc, table, w, bias, offs, out):
         tc.psum_pool(name="pieces", bufs=3) as pieces,
     ):
         rows = held.tile([P, BLOCKS, P], BF16, name="rows")
-        table_blocks = table.rearrange("(b p) k -> p b k", p=P)
+        rows_groups = rows[:].rearrange("p (g j) k -> p g (j k)", j=PAIR)
+        table_groups = table.rearrange("(g p j) k -> p g (j k)", p=P, j=PAIR)
         for c in range(CHUNKS):
-            blocks = slice(c * CHUNK, (c + 1) * CHUNK)
-            nc.sync.dma_start(rows[:, blocks, :], table_blocks[:, blocks, :])
+            groups = slice(c * CHUNK // PAIR, (c + 1) * CHUNK // PAIR)
+            nc.sync.dma_start(rows_groups[:, groups, :], table_groups[:, groups, :])
         offsets = held.tile([P, N // 16], U16, name="offsets")
         nc.sync.dma_start(offsets[:], offs)
 
@@ -39,8 +41,18 @@ def tile_t2gformer_mae_kernel(tc, table, w, bias, offs, out):
         bias_col = held.tile([P, 1], F32, name="bias_col")
         nc.scalar.dma_start(bias_col[:], bias.partition_broadcast(P))
 
-        identity = held.tile([P, P], BF16, name="identity")
-        make_identity(nc, identity[:])
+        spread = [held.tile([P, PAIR * P], BF16, name=f"spread{j}") for j in range(PAIR)]
+        for j in range(PAIR):
+            nc.gpsimd.memset(spread[j][:], 0.0)
+            nc.gpsimd.affine_select(
+                out=spread[j][:],
+                in_=spread[j][:],
+                pattern=[[-1, PAIR * P]],
+                compare_op=NOT_EQUAL,
+                fill=1.0,
+                base=j,
+                channel_multiplier=PAIR,
+            )
         eps_col = held.tile([P, 1], F32, name="eps_col")
         nc.vector.memset(eps_col[:], EPS)
         ones_col = held.tile([P, 1], F32, name="ones_col")
@@ -74,8 +86,13 @@ def tile_t2gformer_mae_kernel(tc, table, w, bias, offs, out):
             for j in range(CHUNK):
                 b = c * CHUNK + j
                 nc.vector.tensor_scalar_mul(unit_rows[:, b, :], rows[:, b, :], rows_rnorm[:, b : b + 1])
+                group = slice((j // PAIR) * PAIR * P, (j // PAIR + 1) * PAIR * P)
                 nc.tensor.matmul(
-                    flipped_chunk[:, j * P : (j + 1) * P], unit_rows[:, b, :], identity[:], start=True, stop=True
+                    flipped_chunk[:, group],
+                    unit_rows[:, b, :],
+                    spread[j % PAIR][:],
+                    start=(j % PAIR == 0),
+                    stop=(j % PAIR == PAIR - 1),
                 )
             nc.vector.tensor_copy(window[:, c * CHUNK * P : (c + 1) * CHUNK * P], flipped_chunk[:])
 

@@ -13,7 +13,6 @@ BLOCKS = S // P
 PAIR = 2
 CHUNK = 4
 CHUNKS = BLOCKS // CHUNK
-VECTOR_CHUNKS = 1
 PIECE = 128
 
 FLOPS = 2 * P * P * N
@@ -70,7 +69,7 @@ def tile_t2gformer_mae_kernel(tc, table, w, bias, offs, out):
         for c in range(CHUNKS):
             blocks = slice(c * CHUNK, (c + 1) * CHUNK)
             for b in range(c * CHUNK, (c + 1) * CHUNK):
-                if c < CHUNKS - VECTOR_CHUNKS:
+                if b % CHUNK < CHUNK - 1:
                     nc.scalar.activation(
                         squares[:, b, :], rows[:, b, :], ACT.Square, accum_out=rows_ss[:, b : b + 1]
                     )

@@ -11,8 +11,9 @@ N = 512
 EPS = 1e-12
 BLOCKS = S // P
 PAIR = 2
-CHUNK = 4
-CHUNKS = BLOCKS // CHUNK
+LOAD = 4
+CHUNK_SIZES = (4, 4, 4, 4, 4, 4, 4, 2, 2)
+assert sum(CHUNK_SIZES) == BLOCKS and all(size % PAIR == 0 for size in CHUNK_SIZES)
 PIECE = 128
 
 FLOPS = 2 * P * P * N
@@ -29,8 +30,8 @@ def tile_t2gformer_mae_kernel(tc, table, w, bias, offs, out):
         rows = held.tile([P, BLOCKS, P], BF16, name="rows")
         rows_groups = rows[:].rearrange("p (g j) k -> p g (j k)", j=PAIR)
         table_groups = table.rearrange("(g p j) k -> p g (j k)", p=P, j=PAIR)
-        for c in range(CHUNKS):
-            groups = slice(c * CHUNK // PAIR, (c + 1) * CHUNK // PAIR)
+        for first in range(0, BLOCKS, LOAD):
+            groups = slice(first // PAIR, (first + LOAD) // PAIR)
             nc.sync.dma_start(rows_groups[:, groups, :], table_groups[:, groups, :])
         offsets = held.tile([P, N // 16], U16, name="offsets")
         nc.sync.dma_start(offsets[:], offs)
@@ -66,10 +67,11 @@ def tile_t2gformer_mae_kernel(tc, table, w, bias, offs, out):
         unit_rows = held.tile([P, BLOCKS, P], BF16, name="unit_rows")
         window = held.tile([P, S], BF16, name="window")
 
-        for c in range(CHUNKS):
-            blocks = slice(c * CHUNK, (c + 1) * CHUNK)
-            for b in range(c * CHUNK, (c + 1) * CHUNK):
-                if b % CHUNK < CHUNK - 1:
+        first = 0
+        for size in CHUNK_SIZES:
+            blocks = slice(first, first + size)
+            for b in range(first, first + size):
+                if b % 4 < 3:
                     nc.scalar.activation(
                         squares[:, b, :], rows[:, b, :], ACT.Square, accum_out=rows_ss[:, b : b + 1]
                     )
@@ -81,9 +83,9 @@ def tile_t2gformer_mae_kernel(tc, table, w, bias, offs, out):
             nc.scalar.activation(
                 rows_rnorm[:, blocks], rows_ss[:, blocks], ACT.Abs_reciprocal_sqrt, bias=eps_col[:]
             )
-            flipped_chunk = flipped.tile([P, CHUNK * P], BF16, name="flipped_chunk")
-            for j in range(CHUNK):
-                b = c * CHUNK + j
+            flipped_chunk = flipped.tile([P, size * P], BF16, name="flipped_chunk")
+            for j in range(size):
+                b = first + j
                 nc.vector.tensor_scalar_mul(unit_rows[:, b, :], rows[:, b, :], rows_rnorm[:, b : b + 1])
                 group = slice((j // PAIR) * PAIR * P, (j // PAIR + 1) * PAIR * P)
                 nc.tensor.matmul(
@@ -93,7 +95,8 @@ def tile_t2gformer_mae_kernel(tc, table, w, bias, offs, out):
                     start=(j % PAIR == 0),
                     stop=(j % PAIR == PAIR - 1),
                 )
-            nc.vector.tensor_copy(window[:, c * CHUNK * P : (c + 1) * CHUNK * P], flipped_chunk[:])
+            nc.vector.tensor_copy(window[:, first * P : (first + size) * P], flipped_chunk[:])
+            first += size
 
         heads_sq = held.tile([P, P], F32, name="heads_sq")
         nc.vector.tensor_tensor(heads_sq[:], heads[:], heads[:], MULT)

@@ -71,7 +71,7 @@ def tile_t2gformer_mae_kernel(tc, table, w, bias, offs, out):
         for size in CHUNK_SIZES:
             blocks = slice(first, first + size)
             for b in range(first, first + size):
-                if b % 4 < 3:
+                if b < first + size - 1:
                     nc.scalar.activation(
                         squares[:, b, :], rows[:, b, :], ACT.Square, accum_out=rows_ss[:, b : b + 1]
                     )

@@ -12,7 +12,7 @@ EPS = 1e-12
 BLOCKS = S // P
 PAIR = 2
 LOAD = 4
-CHUNK_SIZES = (4, 4, 4, 4, 4, 4, 4, 2, 2)
+CHUNK_SIZES = (4, 4, 4, 4, 4, 4, 2, 2, 2, 2)
 assert sum(CHUNK_SIZES) == BLOCKS and all(size % PAIR == 0 for size in CHUNK_SIZES)
 PIECE = 128
 

@@ -1,4 +1,5 @@
 import concourse.mybir as mybir
+from concourse.masks import make_identity
 
 BF16, F32, U16 = mybir.dt.bfloat16, mybir.dt.float32, mybir.dt.uint16
 ACT = mybir.ActivationFunctionType
@@ -14,6 +15,7 @@ PAIR = 2
 LOAD = 4
 CHUNK_SIZES = (4, 4, 4, 4, 4, 4, 2, 2, 2, 2)
 assert sum(CHUNK_SIZES) == BLOCKS and all(size % PAIR == 0 for size in CHUNK_SIZES)
+FIRST_SHORT = 4
 PIECE = 128
 
 FLOPS = 2 * P * P * N
@@ -53,6 +55,8 @@ def tile_t2gformer_mae_kernel(tc, table, w, bias, offs, out):
                 base=j,
                 channel_multiplier=PAIR,
             )
+        identity = held.tile([P, P], BF16, name="identity")
+        make_identity(nc, identity[:])
         eps_col = held.tile([P, 1], F32, name="eps_col")
         nc.vector.memset(eps_col[:], EPS)
         ones_col = held.tile([P, 1], F32, name="ones_col")
@@ -68,7 +72,7 @@ def tile_t2gformer_mae_kernel(tc, table, w, bias, offs, out):
         window = held.tile([P, S], BF16, name="window")
 
         first = 0
-        for size in CHUNK_SIZES:
+        for chunk, size in enumerate(CHUNK_SIZES):
             blocks = slice(first, first + size)
             for b in range(first, first + size):
                 if b < first + size - 1:
@@ -87,15 +91,32 @@ def tile_t2gformer_mae_kernel(tc, table, w, bias, offs, out):
             for j in range(size):
                 b = first + j
                 nc.vector.tensor_scalar_mul(unit_rows[:, b, :], rows[:, b, :], rows_rnorm[:, b : b + 1])
-                group = slice((j // PAIR) * PAIR * P, (j // PAIR + 1) * PAIR * P)
-                nc.tensor.matmul(
-                    flipped_chunk[:, group],
-                    unit_rows[:, b, :],
-                    spread[j % PAIR][:],
-                    start=(j % PAIR == 0),
-                    stop=(j % PAIR == PAIR - 1),
+                if chunk >= FIRST_SHORT:
+                    nc.tensor.matmul(
+                        flipped_chunk[:, j * P : (j + 1) * P],
+                        unit_rows[:, b, :],
+                        identity[:],
+                        start=True,
+                        stop=True,
+                    )
+                else:
+                    group = slice((j // PAIR) * PAIR * P, (j // PAIR + 1) * PAIR * P)
+                    nc.tensor.matmul(
+                        flipped_chunk[:, group],
+                        unit_rows[:, b, :],
+                        spread[j % PAIR][:],
+                        start=(j % PAIR == 0),
+                        stop=(j % PAIR == PAIR - 1),
+                    )
+            columns = slice(first * P, (first + size) * P)
+            copy = nc.scalar.copy if size < LOAD and chunk % 2 == 1 else nc.vector.tensor_copy
+            if chunk >= FIRST_SHORT:
+                copy(
+                    window[:, columns].rearrange("k (g p j) -> k g p j", p=P, j=PAIR),
+                    flipped_chunk[:].rearrange("k (g j p) -> k g p j", p=P, j=PAIR),
                 )
-            nc.vector.tensor_copy(window[:, first * P : (first + size) * P], flipped_chunk[:])
+            else:
+                copy(window[:, columns], flipped_chunk[:])
             first += size
 
         heads_sq = held.tile([P, P], F32, name="heads_sq")
@@ -104,6 +125,9 @@ def tile_t2gformer_mae_kernel(tc, table, w, bias, offs, out):
         nc.tensor.matmul(heads_ss[:], heads_sq[:], ones_col[:], start=True, stop=True)
         heads_rnorm = held.tile([P, 1], F32, name="heads_rnorm")
         nc.scalar.activation(heads_rnorm[:], heads_ss[:], ACT.Abs_reciprocal_sqrt, bias=eps_col[:])
+
+        first_sigmoid = held.tile([P, 1], F32, name="first_sigmoid")
+        nc.scalar.activation(first_sigmoid[:], rows_rnorm[:, BLOCKS - 1 : BLOCKS], ACT.Sigmoid)
 
         probs = held.tile([P, N], F32, name="probs")
         for i in range(N // PIECE):

@@ -10,13 +10,16 @@ P = 128
 S = 4096
 N = 512
 EPS = 1e-12
+PSUM_BANKS = 8
 BLOCKS = S // P
 PAIR = 2
 LOAD = 4
 CHUNK_SIZES = (4, 4, 4, 4, 4, 4, 2, 2, 2, 2)
 assert sum(CHUNK_SIZES) == BLOCKS and all(size % PAIR == 0 for size in CHUNK_SIZES)
 FIRST_SHORT = 4
-PIECE = 128
+
+PIECES = (256, 128, 128)
+assert sum(PIECES) == N
 
 FLOPS = 2 * P * P * N
 
@@ -25,9 +28,8 @@ def tile_t2gformer_mae_kernel(tc, table, w, bias, offs, out):
     nc = tc.nc
     with (
         tc.tile_pool(name="held", bufs=1) as held,
-        tc.psum_pool(name="flipped", bufs=4) as flipped,
-        tc.psum_pool(name="products", bufs=1) as products,
-        tc.psum_pool(name="pieces", bufs=3) as pieces,
+        tc.psum_pool(name="head_bank", bufs=1) as head_bank,
+        tc.psum_pool(name="banks", bufs=PSUM_BANKS - 1) as banks,
     ):
         rows = held.tile([P, BLOCKS, P], BF16, name="rows")
         rows_groups = rows[:].rearrange("p (g j) k -> p g (j k)", j=PAIR)
@@ -87,7 +89,7 @@ def tile_t2gformer_mae_kernel(tc, table, w, bias, offs, out):
             nc.scalar.activation(
                 rows_rnorm[:, blocks], rows_ss[:, blocks], ACT.Abs_reciprocal_sqrt, bias=eps_col[:]
             )
-            flipped_chunk = flipped.tile([P, size * P], BF16, name="flipped_chunk")
+            flipped_chunk = banks.tile([P, size * P], BF16, name="flipped_chunk", tag="bank")
             for j in range(size):
                 b = first + j
                 nc.vector.tensor_scalar_mul(unit_rows[:, b, :], rows[:, b, :], rows_rnorm[:, b : b + 1])
@@ -109,7 +111,7 @@ def tile_t2gformer_mae_kernel(tc, table, w, bias, offs, out):
                         stop=(j % PAIR == PAIR - 1),
                     )
             columns = slice(first * P, (first + size) * P)
-            copy = nc.scalar.copy if size < LOAD and chunk % 2 == 1 else nc.vector.tensor_copy
+            copy = nc.scalar.copy if chunk >= FIRST_SHORT and chunk % 2 == 1 else nc.vector.tensor_copy
             if chunk >= FIRST_SHORT:
                 copy(
                     window[:, columns].rearrange("k (g p j) -> k g p j", p=P, j=PAIR),
@@ -121,22 +123,25 @@ def tile_t2gformer_mae_kernel(tc, table, w, bias, offs, out):
 
         heads_sq = held.tile([P, P], F32, name="heads_sq")
         nc.vector.tensor_tensor(heads_sq[:], heads[:], heads[:], MULT)
-        heads_ss = products.tile([P, 1], F32, name="heads_ss")
+        heads_ss = head_bank.tile([P, 1], F32, name="heads_ss")
         nc.tensor.matmul(heads_ss[:], heads_sq[:], ones_col[:], start=True, stop=True)
         heads_rnorm = held.tile([P, 1], F32, name="heads_rnorm")
         nc.scalar.activation(heads_rnorm[:], heads_ss[:], ACT.Abs_reciprocal_sqrt, bias=eps_col[:])
 
         first_sigmoid = held.tile([P, 1], F32, name="first_sigmoid")
-        nc.scalar.activation(first_sigmoid[:], rows_rnorm[:, BLOCKS - 1 : BLOCKS], ACT.Sigmoid)
+        nc.scalar.activation(
+            first_sigmoid[:], rows_rnorm[:, BLOCKS - 1 : BLOCKS], ACT.Sigmoid, scale=heads_rnorm[:]
+        )
 
         probs = held.tile([P, N], F32, name="probs")
-        for i in range(N // PIECE):
-            columns = slice(i * PIECE, (i + 1) * PIECE)
-            cosines = pieces.tile([P, PIECE], F32, name="cosines")
+        start = 0
+        for piece in PIECES:
+            columns = slice(start, start + piece)
+            cosines = banks.tile([P, piece], F32, name="cosines", tag="bank")
             nc.tensor.matmul(
                 cosines[:],
                 heads[:],
-                window[:].indirect(offsets[:, i * (PIECE // 16) : (i + 1) * (PIECE // 16)]),
+                window[:].indirect(offsets[:, start // 16 : (start + piece) // 16]),
                 start=True,
                 stop=True,
             )
@@ -144,3 +149,4 @@ def tile_t2gformer_mae_kernel(tc, table, w, bias, offs, out):
                 probs[:, columns], cosines[:], ACT.Sigmoid, bias=bias_col[:], scale=heads_rnorm[:]
             )
             nc.sync.dma_start(out[:, columns], probs[:, columns])
+            start += piece

import concourse.mybir as mybir
from concourse.masks import make_identity

BF16, F32, U16 = mybir.dt.bfloat16, mybir.dt.float32, mybir.dt.uint16
ACT = mybir.ActivationFunctionType
MULT = mybir.AluOpType.mult
NOT_EQUAL = mybir.AluOpType.not_equal

P = 128
S = 4096
N = 512
EPS = 1e-12
PSUM_BANKS = 8
BLOCKS = S // P
PAIR = 2
LOAD = 4
CHUNK_SIZES = (4, 4, 4, 4, 4, 4, 2, 2, 2, 2)
assert sum(CHUNK_SIZES) == BLOCKS and all(size % PAIR == 0 for size in CHUNK_SIZES)
FIRST_SHORT = 4

PIECES = (256, 128, 128)
assert sum(PIECES) == N

FLOPS = 2 * P * P * N


def tile_t2gformer_mae_kernel(tc, table, w, bias, offs, out):
    nc = tc.nc
    with (
        tc.tile_pool(name="held", bufs=1) as held,
        tc.psum_pool(name="head_bank", bufs=1) as head_bank,
        tc.psum_pool(name="banks", bufs=PSUM_BANKS - 1) as banks,
    ):
        rows = held.tile([P, BLOCKS, P], BF16, name="rows")
        rows_groups = rows[:].rearrange("p (g j) k -> p g (j k)", j=PAIR)
        table_groups = table.rearrange("(g p j) k -> p g (j k)", p=P, j=PAIR)
        for first in range(0, BLOCKS, LOAD):
            groups = slice(first // PAIR, (first + LOAD) // PAIR)
            nc.sync.dma_start(rows_groups[:, groups, :], table_groups[:, groups, :])
        offsets = held.tile([P, N // 16], U16, name="offsets")
        nc.sync.dma_start(offsets[:], offs)

        heads = held.tile([P, P], BF16, name="heads")
        nc.scalar.dma_start(heads[:], w)
        bias_col = held.tile([P, 1], F32, name="bias_col")
        nc.scalar.dma_start(bias_col[:], bias.partition_broadcast(P))

        spread = [held.tile([P, PAIR * P], BF16, name=f"spread{j}") for j in range(PAIR)]
        for j in range(PAIR):
            nc.gpsimd.memset(spread[j][:], 0.0)
            nc.gpsimd.affine_select(
                out=spread[j][:],
                in_=spread[j][:],
                pattern=[[-1, PAIR * P]],
                compare_op=NOT_EQUAL,
                fill=1.0,
                base=j,
                channel_multiplier=PAIR,
            )
        identity = held.tile([P, P], BF16, name="identity")
        make_identity(nc, identity[:])
        eps_col = held.tile([P, 1], F32, name="eps_col")
        nc.vector.memset(eps_col[:], EPS)
        ones_col = held.tile([P, 1], F32, name="ones_col")
        nc.vector.memset(ones_col[:], 1.0)

        first_root = held.tile([P, 1], F32, name="first_root")
        nc.scalar.activation(first_root[:], ones_col[:], ACT.Abs_reciprocal_sqrt)

        squares = held.tile([P, BLOCKS, P], BF16, name="squares")
        rows_ss = held.tile([P, BLOCKS], F32, name="rows_ss")
        rows_rnorm = held.tile([P, BLOCKS], F32, name="rows_rnorm")
        unit_rows = held.tile([P, BLOCKS, P], BF16, name="unit_rows")
        window = held.tile([P, S], BF16, name="window")

        first = 0
        for chunk, size in enumerate(CHUNK_SIZES):
            blocks = slice(first, first + size)
            for b in range(first, first + size):
                if b < first + size - 1:
                    nc.scalar.activation(
                        squares[:, b, :], rows[:, b, :], ACT.Square, accum_out=rows_ss[:, b : b + 1]
                    )
                else:
                    nc.vector.scalar_tensor_tensor(
                        squares[:, b, :], rows[:, b, :], 1.0, rows[:, b, :], MULT, MULT,
                        accum_out=rows_ss[:, b : b + 1],
                    )
            nc.scalar.activation(
                rows_rnorm[:, blocks], rows_ss[:, blocks], ACT.Abs_reciprocal_sqrt, bias=eps_col[:]
            )
            flipped_chunk = banks.tile([P, size * P], BF16, name="flipped_chunk", tag="bank")
            for j in range(size):
                b = first + j
                nc.vector.tensor_scalar_mul(unit_rows[:, b, :], rows[:, b, :], rows_rnorm[:, b : b + 1])
                if chunk >= FIRST_SHORT:
                    nc.tensor.matmul(
                        flipped_chunk[:, j * P : (j + 1) * P],
                        unit_rows[:, b, :],
                        identity[:],
                        start=True,
                        stop=True,
                    )
                else:
                    group = slice((j // PAIR) * PAIR * P, (j // PAIR + 1) * PAIR * P)
                    nc.tensor.matmul(
                        flipped_chunk[:, group],
                        unit_rows[:, b, :],
                        spread[j % PAIR][:],
                        start=(j % PAIR == 0),
                        stop=(j % PAIR == PAIR - 1),
                    )
            columns = slice(first * P, (first + size) * P)
            copy = nc.scalar.copy if chunk >= FIRST_SHORT and chunk % 2 == 1 else nc.vector.tensor_copy
            if chunk >= FIRST_SHORT:
                copy(
                    window[:, columns].rearrange("k (g p j) -> k g p j", p=P, j=PAIR),
                    flipped_chunk[:].rearrange("k (g j p) -> k g p j", p=P, j=PAIR),
                )
            else:
                copy(window[:, columns], flipped_chunk[:])
            first += size

        heads_sq = held.tile([P, P], F32, name="heads_sq")
        nc.vector.tensor_tensor(heads_sq[:], heads[:], heads[:], MULT)
        heads_ss = head_bank.tile([P, 1], F32, name="heads_ss")
        nc.tensor.matmul(heads_ss[:], heads_sq[:], ones_col[:], start=True, stop=True)
        heads_rnorm = held.tile([P, 1], F32, name="heads_rnorm")
        nc.scalar.activation(heads_rnorm[:], heads_ss[:], ACT.Abs_reciprocal_sqrt, bias=eps_col[:])

        first_sigmoid = held.tile([P, 1], F32, name="first_sigmoid")
        nc.scalar.activation(
            first_sigmoid[:], rows_rnorm[:, BLOCKS - 1 : BLOCKS], ACT.Sigmoid, scale=heads_rnorm[:]
        )

        probs = held.tile([P, N], F32, name="probs")
        start = 0
        for piece in PIECES:
            columns = slice(start, start + piece)
            cosines = banks.tile([P, piece], F32, name="cosines", tag="bank")
            nc.tensor.matmul(
                cosines[:],
                heads[:],
                window[:].indirect(offsets[:, start // 16 : (start + piece) // 16]),
                start=True,
                stop=True,
            )
            nc.scalar.activation(
                probs[:, columns], cosines[:], ACT.Sigmoid, bias=bias_col[:], scale=heads_rnorm[:]
            )
            nc.sync.dma_start(out[:, columns], probs[:, columns])
            start += piece
